import numpy as np
import ml_dtypes


def mxq(x, axis, fmt="e4m3"):
    dtype, down = {"e4m3": (ml_dtypes.float8_e4m3fn, 7), "e5m2": (ml_dtypes.float8_e5m2, 14)}[fmt]
    v = np.moveaxis(np.asarray(x, np.float32).astype(ml_dtypes.bfloat16).astype(np.float64), axis, -1)
    blocks = v.reshape(v.shape[:-1] + (-1, 32))
    amax = np.abs(blocks).max(-1, keepdims=True)
    byte = np.maximum(np.where(amax > 0, np.frexp(amax)[1] - 1 + 127, 0) - down, 1)
    scale = np.exp2(byte - 127.0)
    codes = (blocks / scale).astype(np.float32).astype(dtype).astype(np.float64)
    return np.moveaxis((codes * scale).reshape(v.shape), -1, axis)


WIDE = False


def mx_kscale(k):
    if not WIDE:
        return np.ones(k)
    levels = np.array([10, -10, 5, -5, 0])
    if k % 512:
        return np.exp2(np.random.permutation(np.resize(levels, k // 32))).repeat(32)
    a = np.empty((k // 512, 16))
    for p in range(k // 512):
        a[p, :8] = np.random.permutation(np.resize(levels, 8))
        for g in range(8):
            far = levels[np.abs(levels - a[p, g]) >= 10]
            a[p, g + 8] = far[np.random.randint(len(far))]
    return np.exp2(a.ravel()).repeat(32)


BF16 = ml_dtypes.bfloat16


def bf(x):
    return np.asarray(x, np.float32).astype(BF16)


def f64(x):
    return np.asarray(x).astype(np.float64)


N, IN_F, OUT_F = 512, 1024, 128
POW = 2


def setup_inputs():
    s = mx_kscale(IN_F)
    u = np.exp2(np.round(np.log2(mx_kscale(N)) / 2))
    return {"input": bf(np.random.standard_normal((N, IN_F)) * s / (u * u)[:, None]),
            "adj": bf(np.random.uniform(0.0, 1.0, (N, N)) * 1.5 / N ** 0.25 * u),
            "weight": bf(np.random.uniform(-1.0, 1.0, (IN_F, OUT_F)) * 1.7 / np.sqrt(IN_F) / s[:, None]),
            "bias": bf(np.random.standard_normal(OUT_F) * 0.3)}


def reference(input, adj, weight, bias):
    k_adj = f64(adj) ** POW
    support = mxq(f64(input), 1, "e4m3") @ mxq(f64(weight), 0, "e4m3")
    out = (mxq(k_adj, 1, "e4m3") @ mxq(support, 0, "e4m3")) + f64(bias)
    return np.where(out > 0, out, np.expm1(out))

@@ -1,0 +1,208 @@
+from contextlib import ExitStack
+
+import concourse.mybir as mybir
+from concourse.masks import make_identity
+
+F32 = mybir.dt.float32
+BF16 = mybir.dt.bfloat16
+U32 = mybir.dt.uint32
+U8 = mybir.dt.uint8
+FP8X4 = mybir.dt.float8_e4m3fn_x4
+ACT = mybir.ActivationFunctionType
+ALU = mybir.AluOpType
+
+P = 128
+PACK = 4
+HALVES = 2
+PAIR = 2
+NODES = 512
+IN_F = 1024
+OUT_F = 128
+K_PASS = P * PACK
+PASSES = IN_F // K_PASS
+TILES = NODES // P
+
+W_SLOT = 2
+FIRST_PIECES = 2
+
+FLOPS = 2 * NODES * IN_F * OUT_F + 2 * NODES * NODES * OUT_F
+
+
+def tile_netgraphconvolution_s_kernel(tc, x, adj, weight, bias, out):
+    nc = tc.nc
+    with ExitStack() as ctx:
+        keep = ctx.enter_context(tc.tile_pool(name="keep", bufs=1))
+        turned = ctx.enter_context(tc.psum_pool(name="turned", bufs=4))
+        sums = ctx.enter_context(tc.psum_pool(name="sums", bufs=1))
+        ctx.enter_context(tc.manual_schedule())
+
+        ident = keep.tile([P, P], F32)
+        make_identity(nc, ident[:])
+        warm_in = keep.tile([P, 1], F32)
+        warm_out = keep.tile([P, 1], F32)
+        nc.vector.memset(warm_in[:], 0.0)
+        bias_rows = keep.tile([P, OUT_F], BF16)
+        nc.vector.memset(bias_rows[:], 0.0)
+        ones = keep.tile([P, P], BF16)
+        nc.vector.memset(ones[:], 1.0)
+        nc.scalar.dma_start(out=bias_rows[0:1, :], in_=bias.rearrange("(o f) -> o f", o=1))
+        nc.scalar.activation(out=warm_out[:], in_=warm_in[:], func=ACT.Exp)
+
+        x_tiles = x.rearrange("(p t) k -> t p k", t=TILES)
+        x_rows = []
+        for t in range(TILES):
+            x_t = keep.tile([P, IN_F], BF16, name="x_rows%d" % t)
+            x_rows.append(x_t)
+        for t in range(TILES):
+            pieces = FIRST_PIECES if t == 0 else 1
+            width = IN_F // pieces
+            for c in range(pieces):
+                cols = slice(c * width, (c + 1) * width)
+                nc.sync.dma_start(out=x_rows[t][:, cols], in_=x_tiles[t][:, cols])
+        w_raw = keep.tile([P, PASSES, PACK, OUT_F], BF16)
+        nc.sync.dma_start(
+            out=w_raw[:].rearrange("p g t c -> p g (t c)"),
+            in_=weight.rearrange("(g p t) c -> p g (t c)", g=PASSES, p=P),
+        )
+        adj_blocks = adj.rearrange("(p b) j -> p b j", b=TILES)
+        adj_rows = []
+        for h in range(TILES // PAIR):
+            adj_h = keep.tile([P, PAIR, NODES], BF16, name="adj_rows%d" % h)
+            nc.sync.dma_start(out=adj_h[:], in_=adj_blocks[:, PAIR * h : PAIR * h + PAIR, :])
+            adj_rows.append(adj_h)
+
+        w_grouped = keep.tile([P, PASSES, OUT_F, PACK], BF16, align_bytes=64)
+        w_codes = keep.tile([P, PASSES, OUT_F], U32, align_bytes=64)
+        w_scales = keep.tile([P, PASSES, OUT_F], U8, align_bytes=64)
+
+        def quantise_weight():
+            nc.vector.tensor_copy(out=w_grouped[:], in_=w_raw[:].rearrange("p g t c -> p g c t"))
+            nc.vector.quantize_mx(
+                out=w_codes[:].rearrange("p g c -> p (g c)").bitcast(FP8X4),
+                scales=w_scales[:].rearrange("p g c -> p (g c)"),
+                in_=w_grouped[:].rearrange("p g c t -> p (g c t)"),
+            )
+
+        x_codes = keep.tile([P, TILES, PASSES, P], U32, align_bytes=64)
+        x_scales = keep.tile([P, TILES, PASSES, P], U8, align_bytes=64)
+        x_grouped = []
+        for t in range(TILES):
+            x_g = keep.tile([P, PASSES * P * PACK], BF16, name="x_grouped%d" % t, align_bytes=64)
+            x_grouped.append(x_g)
+
+        def turn_x(t):
+            x_words = x_rows[t][:].bitcast(F32)
+            xT = turned.tile([P, PASSES * HALVES, P], F32, tag="turned")
+            for g in range(PASSES):
+                for u in range(HALVES):
+                    first = HALVES * P * g + u
+                    nc.tensor.transpose(
+                        xT[:, HALVES * g + u, :], x_words[:, first : HALVES * P * (g + 1) : HALVES], ident[:]
+                    )
+            grouped_words = x_grouped[t][:].bitcast(F32).rearrange("p (g n u) -> p g n u", g=PASSES, u=HALVES)
+            turned_words = xT[:].rearrange("p (g u) n -> p g n u", g=PASSES)
+            nc.scalar.copy(out=grouped_words, in_=turned_words)
+
+        def quantise_x(t):
+            nc.vector.quantize_mx(
+                out=x_codes[:, t].rearrange("p g n -> p (g n)").bitcast(FP8X4),
+                scales=x_scales[:, t].rearrange("p g n -> p (g n)"),
+                in_=x_grouped[t][:],
+            )
+
+        for t in range(TILES):
+            turn_x(t)
+            if t == W_SLOT:
+                quantise_weight()
+            quantise_x(t)
+
+        a_codes = keep.tile([P, TILES, P], U32, align_bytes=64)
+        a_scales = keep.tile([P, TILES, P], U8, align_bytes=64)
+        adj_turned = []
+        for b in range(TILES):
+            aT = turned.tile([P, HALVES, P], F32, tag="turned")
+            adj_words = adj_rows[b // PAIR][:, b % PAIR, :].bitcast(F32)
+            for u in range(HALVES):
+                nc.tensor.transpose(aT[:, u, :], adj_words[:, u : HALVES * P : HALVES], ident[:])
+            adj_turned.append(aT)
+
+        def square_and_quantise(b):
+            a_grouped = keep.tile([P, P * PACK], BF16, name="a_grouped%d" % b, align_bytes=64)
+            nc.scalar.activation(
+                out=a_grouped[:].rearrange("p (i u e) -> p i u e", u=HALVES, e=PAIR),
+                in_=adj_turned[b][:].bitcast(BF16).rearrange("p u (i e) -> p i u e", e=PAIR),
+                func=ACT.Square,
+            )
+            nc.vector.quantize_mx(
+                out=a_codes[:, b, :].bitcast(FP8X4), scales=a_scales[:, b, :], in_=a_grouped[:]
+            )
+
+        square_and_quantise(0)
+        square_and_quantise(1)
+
+        sup_ps = sums.tile([P, TILES, OUT_F], F32)
+        for t in range(TILES):
+            for g in range(PASSES):
+                nc.tensor.matmul_mx(
+                    out=sup_ps[:, t, :],
+                    lhsT=x_codes[:, t, g, :].bitcast(FP8X4),
+                    lhsT_scale=x_scales[:, t, g, :],
+                    rhs=w_codes[:, g, :].bitcast(FP8X4),
+                    rhs_scale=w_scales[:, g, :],
+                    start=(g == 0),
+                    stop=(g == PASSES - 1),
+                )
+        bias_ps = sums.tile([P, OUT_F], F32)
+        nc.tensor.matmul(out=bias_ps[:], lhsT=ones[:], rhs=bias_rows[:], start=True, stop=True)
+        bias_all = keep.tile([P, OUT_F], F32)
+        sup_grouped = keep.tile([P, OUT_F, PACK], BF16, align_bytes=64)
+        nc.vector.tensor_copy(out=sup_grouped[:], in_=sup_ps[:].rearrange("p t f -> p f t"))
+        sup_codes = keep.tile([P, OUT_F], U32, align_bytes=64)
+        sup_scales = keep.tile([P, OUT_F], U8, align_bytes=64)
+        nc.vector.quantize_mx(
+            out=sup_codes[:].bitcast(FP8X4),
+            scales=sup_scales[:],
+            in_=sup_grouped[:].rearrange("p f t -> p (f t)"),
+        )
+
+        square_and_quantise(2)
+        square_and_quantise(3)
+        nc.scalar.copy(out=bias_all[:], in_=bias_ps[:])
+
+        out_blocks = out.rearrange("(p b) f -> p b f", b=TILES)
+        z = []
+        e = []
+        for h in range(TILES // PAIR):
+            out_ps = sums.tile([P, PAIR, OUT_F], F32, name="out_ps%d" % h)
+            for s in range(PAIR):
+                b = PAIR * h + s
+                nc.tensor.matmul_mx(
+                    out=out_ps[:, s, :],
+                    lhsT=a_codes[:, b, :].bitcast(FP8X4),
+                    lhsT_scale=a_scales[:, b, :],
+                    rhs=sup_codes[:].bitcast(FP8X4),
+                    rhs_scale=sup_scales[:],
+                    start=True,
+                    stop=True,
+                )
+            z_h = keep.tile([P, PAIR, OUT_F], F32, name="z%d" % h)
+            nc.vector.tensor_tensor(
+                out=z_h[:], in0=out_ps[:], in1=bias_all[:].unsqueeze(1).to_broadcast([P, PAIR, OUT_F]), op=ALU.add
+            )
+            e_h = keep.tile([P, PAIR, OUT_F], F32, name="e%d" % h)
+            nc.scalar.activation(out=e_h[:], in_=z_h[:], func=ACT.Exp)
+            z.append(z_h)
+            e.append(e_h)
+        for h in range(TILES // PAIR):
+            r = keep.tile([P, PAIR, OUT_F], F32, name="r%d" % h)
+            nc.vector.tensor_scalar(out=r[:], in0=z[h][:], scalar1=0.0, scalar2=-1.0, op0=ALU.max, op1=ALU.add)
+            res = keep.tile([P, PAIR, OUT_F], F32, name="res%d" % h)
+            nc.vector.scalar_tensor_tensor(
+                out=res[:].rearrange("p b f -> p (b f)"),
+                in0=e[h][:].rearrange("p b f -> p (b f)"),
+                scalar=1.0,
+                in1=r[:].rearrange("p b f -> p (b f)"),
+                op0=ALU.min,
+                op1=ALU.add,
+            )
+            nc.sync.dma_start(out=out_blocks[:, PAIR * h : PAIR * h + PAIR, :], in_=res[:])

@@ -75,8 +75,10 @@ def tile_netgraphconvolution_s_kernel(tc, x, adj, weight, bias, out):
         w_codes = keep.tile([P, PASSES, OUT_F], U32, align_bytes=64)
         w_scales = keep.tile([P, PASSES, OUT_F], U8, align_bytes=64)
 
-        def quantise_weight():
+        def group_weight():
             nc.vector.tensor_copy(out=w_grouped[:], in_=w_raw[:].rearrange("p g t c -> p g c t"))
+
+        def quantise_weight():
             nc.vector.quantize_mx(
                 out=w_codes[:].rearrange("p g c -> p (g c)").bitcast(FP8X4),
                 scales=w_scales[:].rearrange("p g c -> p (g c)"),
@@ -113,8 +115,10 @@ def tile_netgraphconvolution_s_kernel(tc, x, adj, weight, bias, out):
         for t in range(TILES):
             turn_x(t)
             if t == W_SLOT:
-                quantise_weight()
+                group_weight()
             quantise_x(t)
+            if t == W_SLOT:
+                quantise_weight()
 
         a_codes = keep.tile([P, TILES, P], U32, align_bytes=64)
         a_scales = keep.tile([P, TILES, P], U8, align_bytes=64)
@@ -193,15 +197,18 @@ def tile_netgraphconvolution_s_kernel(tc, x, adj, weight, bias, out):
             nc.scalar.activation(out=e_h[:], in_=z_h[:], func=ACT.Exp)
             z.append(z_h)
             e.append(e_h)
+        r = []
         for h in range(TILES // PAIR):
-            r = keep.tile([P, PAIR, OUT_F], F32, name="r%d" % h)
-            nc.vector.tensor_scalar(out=r[:], in0=z[h][:], scalar1=0.0, scalar2=-1.0, op0=ALU.max, op1=ALU.add)
+            r_h = keep.tile([P, PAIR, OUT_F], F32, name="r%d" % h)
+            nc.vector.tensor_scalar(out=r_h[:], in0=z[h][:], scalar1=0.0, scalar2=-1.0, op0=ALU.max, op1=ALU.add)
+            r.append(r_h)
+        for h in range(TILES // PAIR):
             res = keep.tile([P, PAIR, OUT_F], F32, name="res%d" % h)
             nc.vector.scalar_tensor_tensor(
                 out=res[:].rearrange("p b f -> p (b f)"),
                 in0=e[h][:].rearrange("p b f -> p (b f)"),
                 scalar=1.0,
-                in1=r[:].rearrange("p b f -> p (b f)"),
+                in1=r[h][:].rearrange("p b f -> p (b f)"),
                 op0=ALU.min,
                 op1=ALU.add,
             )

@@ -22,7 +22,7 @@ K_PASS = P * PACK
 PASSES = IN_F // K_PASS
 TILES = NODES // P
 
-W_SLOT = 2
+W_SLOT = 1
 FIRST_PIECES = 2
 
 FLOPS = 2 * NODES * IN_F * OUT_F + 2 * NODES * NODES * OUT_F
@@ -112,6 +112,8 @@ def tile_netgraphconvolution_s_kernel(tc, x, adj, weight, bias, out):
                 in_=x_grouped[t][:],
             )
 
+        bias_ps = sums.tile([P, OUT_F], F32)
+        bias_all = keep.tile([P, OUT_F], F32)
         for t in range(TILES):
             turn_x(t)
             if t == W_SLOT:
@@ -119,30 +121,47 @@ def tile_netgraphconvolution_s_kernel(tc, x, adj, weight, bias, out):
             quantise_x(t)
             if t == W_SLOT:
                 quantise_weight()
+        nc.tensor.matmul(out=bias_ps[:], lhsT=ones[:], rhs=bias_rows[:], start=True, stop=True)
+        nc.vector.tensor_copy(out=bias_all[:], in_=bias_ps[:])
 
         a_codes = keep.tile([P, TILES, P], U32, align_bytes=64)
         a_scales = keep.tile([P, TILES, P], U8, align_bytes=64)
         adj_turned = []
-        for b in range(TILES):
+
+        def turn_adj(b, rows):
             aT = turned.tile([P, HALVES, P], F32, tag="turned")
-            adj_words = adj_rows[b // PAIR][:, b % PAIR, :].bitcast(F32)
+            adj_words = rows.bitcast(F32)
             for u in range(HALVES):
                 nc.tensor.transpose(aT[:, u, :], adj_words[:, u : HALVES * P : HALVES], ident[:])
             adj_turned.append(aT)
 
-        def square_and_quantise(b):
-            a_grouped = keep.tile([P, P * PACK], BF16, name="a_grouped%d" % b, align_bytes=64)
+        a_grouped = []
+        for b in range(TILES):
+            a_g = keep.tile([P, P * PACK], BF16, name="a_grouped%d" % b, align_bytes=64)
+            a_grouped.append(a_g)
+
+        def square(b):
             nc.scalar.activation(
-                out=a_grouped[:].rearrange("p (i u e) -> p i u e", u=HALVES, e=PAIR),
+                out=a_grouped[b][:].rearrange("p (i u e) -> p i u e", u=HALVES, e=PAIR),
                 in_=adj_turned[b][:].bitcast(BF16).rearrange("p u (i e) -> p i u e", e=PAIR),
                 func=ACT.Square,
             )
+
+        def quantise_adj(b):
             nc.vector.quantize_mx(
-                out=a_codes[:, b, :].bitcast(FP8X4), scales=a_scales[:, b, :], in_=a_grouped[:]
+                out=a_codes[:, b, :].bitcast(FP8X4), scales=a_scales[:, b, :], in_=a_grouped[b][:]
             )
 
-        square_and_quantise(0)
-        square_and_quantise(1)
+        def adj_block(b):
+            return adj_rows[b // PAIR][:, b % PAIR, :]
+
+        for b in range(PAIR):
+            turn_adj(b, adj_block(b))
+            square(b)
+        last = TILES - 1
+        squared = keep.tile([P, NODES], BF16)
+        nc.vector.tensor_tensor(out=squared[:], in0=adj_block(last), in1=adj_block(last), op=ALU.mult)
+        quantise_adj(0)
 
         sup_ps = sums.tile([P, TILES, OUT_F], F32)
         for t in range(TILES):
@@ -156,11 +175,16 @@ def tile_netgraphconvolution_s_kernel(tc, x, adj, weight, bias, out):
                     start=(g == 0),
                     stop=(g == PASSES - 1),
                 )
-        bias_ps = sums.tile([P, OUT_F], F32)
-        nc.tensor.matmul(out=bias_ps[:], lhsT=ones[:], rhs=bias_rows[:], start=True, stop=True)
-        bias_all = keep.tile([P, OUT_F], F32)
+        turn_adj(PAIR, adj_block(PAIR))
+        square(PAIR)
+        turn_adj(last, squared[:])
+        nc.scalar.copy(
+            out=a_grouped[last][:].bitcast(F32).rearrange("p (i u) -> p i u", u=HALVES),
+            in_=adj_turned[last][:].rearrange("p u i -> p i u"),
+        )
         sup_grouped = keep.tile([P, OUT_F, PACK], BF16, align_bytes=64)
         nc.vector.tensor_copy(out=sup_grouped[:], in_=sup_ps[:].rearrange("p t f -> p f t"))
+        quantise_adj(1)
         sup_codes = keep.tile([P, OUT_F], U32, align_bytes=64)
         sup_scales = keep.tile([P, OUT_F], U8, align_bytes=64)
         nc.vector.quantize_mx(
@@ -169,9 +193,8 @@ def tile_netgraphconvolution_s_kernel(tc, x, adj, weight, bias, out):
             in_=sup_grouped[:].rearrange("p f t -> p (f t)"),
         )
 
-        square_and_quantise(2)
-        square_and_quantise(3)
-        nc.scalar.copy(out=bias_all[:], in_=bias_ps[:])
+        quantise_adj(2)
+        quantise_adj(3)
 
         out_blocks = out.rearrange("(p b) f -> p b f", b=TILES)
         z = []

@@ -23,6 +23,7 @@ PASSES = IN_F // K_PASS
 TILES = NODES // P
 
 W_SLOT = 1
+WARM_UPS = 3
 FIRST_PIECES = 2
 
 FLOPS = 2 * NODES * IN_F * OUT_F + 2 * NODES * NODES * OUT_F
@@ -114,6 +115,8 @@ def tile_netgraphconvolution_s_kernel(tc, x, adj, weight, bias, out):
 
         bias_ps = sums.tile([P, OUT_F], F32)
         bias_all = keep.tile([P, OUT_F], F32)
+        for i in range(WARM_UPS):
+            nc.tensor.matmul(out=bias_ps[:], lhsT=ident[:], rhs=ident[:], start=True, stop=True)
         for t in range(TILES):
             turn_x(t)
             if t == W_SLOT:
@@ -122,7 +125,6 @@ def tile_netgraphconvolution_s_kernel(tc, x, adj, weight, bias, out):
             if t == W_SLOT:
                 quantise_weight()
         nc.tensor.matmul(out=bias_ps[:], lhsT=ones[:], rhs=bias_rows[:], start=True, stop=True)
-        nc.vector.tensor_copy(out=bias_all[:], in_=bias_ps[:])
 
         a_codes = keep.tile([P, TILES, P], U32, align_bytes=64)
         a_scales = keep.tile([P, TILES, P], U8, align_bytes=64)
@@ -158,6 +160,8 @@ def tile_netgraphconvolution_s_kernel(tc, x, adj, weight, bias, out):
         for b in range(PAIR):
             turn_adj(b, adj_block(b))
             square(b)
+        turn_adj(PAIR, adj_block(PAIR))
+        square(PAIR)
         last = TILES - 1
         squared = keep.tile([P, NODES], BF16)
         nc.vector.tensor_tensor(out=squared[:], in0=adj_block(last), in1=adj_block(last), op=ALU.mult)
@@ -175,8 +179,6 @@ def tile_netgraphconvolution_s_kernel(tc, x, adj, weight, bias, out):
                     start=(g == 0),
                     stop=(g == PASSES - 1),
                 )
-        turn_adj(PAIR, adj_block(PAIR))
-        square(PAIR)
         turn_adj(last, squared[:])
         nc.scalar.copy(
             out=a_grouped[last][:].bitcast(F32).rearrange("p (i u) -> p i u", u=HALVES),
@@ -194,6 +196,7 @@ def tile_netgraphconvolution_s_kernel(tc, x, adj, weight, bias, out):
         )
 
         quantise_adj(2)
+        nc.vector.tensor_copy(out=bias_all[:], in_=bias_ps[:])
         quantise_adj(3)
 
         out_blocks = out.rearrange("(p b) f -> p b f", b=TILES)

@@ -22,8 +22,7 @@ K_PASS = P * PACK
 PASSES = IN_F // K_PASS
 TILES = NODES // P
 
-W_SLOT = 1
-WARM_UPS = 3
+W_SLOT = 2
 FIRST_PIECES = 2
 
 FLOPS = 2 * NODES * IN_F * OUT_F + 2 * NODES * NODES * OUT_F
@@ -46,7 +45,6 @@ def tile_netgraphconvolution_s_kernel(tc, x, adj, weight, bias, out):
         nc.vector.memset(bias_rows[:], 0.0)
         ones = keep.tile([P, P], BF16)
         nc.vector.memset(ones[:], 1.0)
-        nc.scalar.dma_start(out=bias_rows[0:1, :], in_=bias.rearrange("(o f) -> o f", o=1))
         nc.scalar.activation(out=warm_out[:], in_=warm_in[:], func=ACT.Exp)
 
         x_tiles = x.rearrange("(p t) k -> t p k", t=TILES)
@@ -71,6 +69,7 @@ def tile_netgraphconvolution_s_kernel(tc, x, adj, weight, bias, out):
             adj_h = keep.tile([P, PAIR, NODES], BF16, name="adj_rows%d" % h)
             nc.sync.dma_start(out=adj_h[:], in_=adj_blocks[:, PAIR * h : PAIR * h + PAIR, :])
             adj_rows.append(adj_h)
+        nc.sync.dma_start(out=bias_rows[0:1, :], in_=bias.rearrange("(o f) -> o f", o=1))
 
         w_grouped = keep.tile([P, PASSES, OUT_F, PACK], BF16, align_bytes=64)
         w_codes = keep.tile([P, PASSES, OUT_F], U32, align_bytes=64)
@@ -115,8 +114,6 @@ def tile_netgraphconvolution_s_kernel(tc, x, adj, weight, bias, out):
 
         bias_ps = sums.tile([P, OUT_F], F32)
         bias_all = keep.tile([P, OUT_F], F32)
-        for i in range(WARM_UPS):
-            nc.tensor.matmul(out=bias_ps[:], lhsT=ident[:], rhs=ident[:], start=True, stop=True)
         for t in range(TILES):
             turn_x(t)
             if t == W_SLOT:
@@ -124,7 +121,6 @@ def tile_netgraphconvolution_s_kernel(tc, x, adj, weight, bias, out):
             quantise_x(t)
             if t == W_SLOT:
                 quantise_weight()
-        nc.tensor.matmul(out=bias_ps[:], lhsT=ones[:], rhs=bias_rows[:], start=True, stop=True)
 
         a_codes = keep.tile([P, TILES, P], U32, align_bytes=64)
         a_scales = keep.tile([P, TILES, P], U8, align_bytes=64)
@@ -179,6 +175,7 @@ def tile_netgraphconvolution_s_kernel(tc, x, adj, weight, bias, out):
                     start=(g == 0),
                     stop=(g == PASSES - 1),
                 )
+        nc.tensor.matmul(out=bias_ps[:], lhsT=ones[:], rhs=bias_rows[:], start=True, stop=True)
         turn_adj(last, squared[:])
         nc.scalar.copy(
             out=a_grouped[last][:].bitcast(F32).rearrange("p (i u) -> p i u", u=HALVES),

@@ -23,13 +23,13 @@ PASSES = IN_F // K_PASS
 TILES = NODES // P
 
 W_SLOT = 2
-FIRST_PIECES = 2
 
 FLOPS = 2 * NODES * IN_F * OUT_F + 2 * NODES * NODES * OUT_F
 
 
 def tile_netgraphconvolution_s_kernel(tc, x, adj, weight, bias, out):
     nc = tc.nc
+    last = TILES - 1
     with ExitStack() as ctx:
         keep = ctx.enter_context(tc.tile_pool(name="keep", bufs=1))
         turned = ctx.enter_context(tc.psum_pool(name="turned", bufs=4))
@@ -52,23 +52,30 @@ def tile_netgraphconvolution_s_kernel(tc, x, adj, weight, bias, out):
         for t in range(TILES):
             x_t = keep.tile([P, IN_F], BF16, name="x_rows%d" % t)
             x_rows.append(x_t)
-        for t in range(TILES):
-            pieces = FIRST_PIECES if t == 0 else 1
+        w_raw = keep.tile([P, PASSES, PACK, OUT_F], BF16)
+        adj_blocks = adj.rearrange("(p b) j -> p b j", b=TILES)
+        adj_rows = keep.tile([P, TILES, NODES], BF16)
+
+        def load_x(t):
+            pieces = 1 if 0 < t < last else PASSES
             width = IN_F // pieces
             for c in range(pieces):
                 cols = slice(c * width, (c + 1) * width)
                 nc.sync.dma_start(out=x_rows[t][:, cols], in_=x_tiles[t][:, cols])
-        w_raw = keep.tile([P, PASSES, PACK, OUT_F], BF16)
+
+        def load_adj(blocks):
+            nc.sync.dma_start(out=adj_rows[:, blocks, :], in_=adj_blocks[:, blocks, :])
+
+        for t in range(last):
+            load_x(t)
+        load_adj(slice(0, 1))
         nc.sync.dma_start(
             out=w_raw[:].rearrange("p g t c -> p g (t c)"),
             in_=weight.rearrange("(g p t) c -> p g (t c)", g=PASSES, p=P),
         )
-        adj_blocks = adj.rearrange("(p b) j -> p b j", b=TILES)
-        adj_rows = []
-        for h in range(TILES // PAIR):
-            adj_h = keep.tile([P, PAIR, NODES], BF16, name="adj_rows%d" % h)
-            nc.sync.dma_start(out=adj_h[:], in_=adj_blocks[:, PAIR * h : PAIR * h + PAIR, :])
-            adj_rows.append(adj_h)
+        load_x(last)
+        load_adj(slice(1, last))
+        load_adj(slice(last, TILES))
         nc.sync.dma_start(out=bias_rows[0:1, :], in_=bias.rearrange("(o f) -> o f", o=1))
 
         w_grouped = keep.tile([P, PASSES, OUT_F, PACK], BF16, align_bytes=64)
@@ -92,46 +99,39 @@ def tile_netgraphconvolution_s_kernel(tc, x, adj, weight, bias, out):
             x_g = keep.tile([P, PASSES * P * PACK], BF16, name="x_grouped%d" % t, align_bytes=64)
             x_grouped.append(x_g)
 
-        def turn_x(t):
+        def turn_x(t, g0, g1):
             x_words = x_rows[t][:].bitcast(F32)
-            xT = turned.tile([P, PASSES * HALVES, P], F32, tag="turned")
-            for g in range(PASSES):
+            xT = turned.tile([P, (g1 - g0) * HALVES, P], F32, tag="turned")
+            for g in range(g0, g1):
                 for u in range(HALVES):
                     first = HALVES * P * g + u
                     nc.tensor.transpose(
-                        xT[:, HALVES * g + u, :], x_words[:, first : HALVES * P * (g + 1) : HALVES], ident[:]
+                        xT[:, HALVES * (g - g0) + u, :], x_words[:, first : HALVES * P * (g + 1) : HALVES], ident[:]
                     )
             grouped_words = x_grouped[t][:].bitcast(F32).rearrange("p (g n u) -> p g n u", g=PASSES, u=HALVES)
-            turned_words = xT[:].rearrange("p (g u) n -> p g n u", g=PASSES)
-            nc.scalar.copy(out=grouped_words, in_=turned_words)
+            turned_words = xT[:].rearrange("p (g u) n -> p g n u", u=HALVES)
+            nc.scalar.copy(out=grouped_words[:, g0:g1], in_=turned_words)
 
-        def quantise_x(t):
+        def quantise_x(t, g0, g1):
             nc.vector.quantize_mx(
-                out=x_codes[:, t].rearrange("p g n -> p (g n)").bitcast(FP8X4),
-                scales=x_scales[:, t].rearrange("p g n -> p (g n)"),
-                in_=x_grouped[t][:],
+                out=x_codes[:, t, g0:g1].rearrange("p g n -> p (g n)").bitcast(FP8X4),
+                scales=x_scales[:, t, g0:g1].rearrange("p g n -> p (g n)"),
+                in_=x_grouped[t][:, g0 * P * PACK : g1 * P * PACK],
             )
 
         bias_ps = sums.tile([P, OUT_F], F32)
         bias_all = keep.tile([P, OUT_F], F32)
-        for t in range(TILES):
-            turn_x(t)
-            if t == W_SLOT:
-                group_weight()
-            quantise_x(t)
-            if t == W_SLOT:
-                quantise_weight()
 
         a_codes = keep.tile([P, TILES, P], U32, align_bytes=64)
         a_scales = keep.tile([P, TILES, P], U8, align_bytes=64)
-        adj_turned = []
+        adj_turned = {}
 
         def turn_adj(b, rows):
             aT = turned.tile([P, HALVES, P], F32, tag="turned")
             adj_words = rows.bitcast(F32)
             for u in range(HALVES):
                 nc.tensor.transpose(aT[:, u, :], adj_words[:, u : HALVES * P : HALVES], ident[:])
-            adj_turned.append(aT)
+            adj_turned[b] = aT
 
         a_grouped = []
         for b in range(TILES):
@@ -151,14 +151,22 @@ def tile_netgraphconvolution_s_kernel(tc, x, adj, weight, bias, out):
             )
 
         def adj_block(b):
-            return adj_rows[b // PAIR][:, b % PAIR, :]
+            return adj_rows[:, b, :]
 
-        for b in range(PAIR):
+        for t in range(last):
+            turn_x(t, 0, PASSES)
+            if t == W_SLOT:
+                group_weight()
+            quantise_x(t, 0, PASSES)
+        turn_adj(0, adj_block(0))
+        square(0)
+        quantise_weight()
+        for g in range(PASSES):
+            turn_x(last, g, g + 1)
+            quantise_x(last, g, g + 1)
+        for b in range(1, last):
             turn_adj(b, adj_block(b))
             square(b)
-        turn_adj(PAIR, adj_block(PAIR))
-        square(PAIR)
-        last = TILES - 1
         squared = keep.tile([P, NODES], BF16)
         nc.vector.tensor_tensor(out=squared[:], in0=adj_block(last), in1=adj_block(last), op=ALU.mult)
         quantise_adj(0)

@@ -22,7 +22,7 @@ K_PASS = P * PACK
 PASSES = IN_F // K_PASS
 TILES = NODES // P
 
-W_SLOT = 2
+W_SLOT = 1
 
 FLOPS = 2 * NODES * IN_F * OUT_F + 2 * NODES * NODES * OUT_F
 
@@ -68,15 +68,14 @@ def tile_netgraphconvolution_s_kernel(tc, x, adj, weight, bias, out):
 
         for t in range(last):
             load_x(t)
-        load_adj(slice(0, 1))
         nc.sync.dma_start(
             out=w_raw[:].rearrange("p g t c -> p g (t c)"),
             in_=weight.rearrange("(g p t) c -> p g (t c)", g=PASSES, p=P),
         )
         load_x(last)
-        load_adj(slice(1, last))
-        load_adj(slice(last, TILES))
         nc.sync.dma_start(out=bias_rows[0:1, :], in_=bias.rearrange("(o f) -> o f", o=1))
+        for h in range(TILES // PAIR):
+            load_adj(slice(PAIR * h, PAIR * h + PAIR))
 
         w_grouped = keep.tile([P, PASSES, OUT_F, PACK], BF16, align_bytes=64)
         w_codes = keep.tile([P, PASSES, OUT_F], U32, align_bytes=64)
@@ -145,30 +144,34 @@ def tile_netgraphconvolution_s_kernel(tc, x, adj, weight, bias, out):
                 func=ACT.Square,
             )
 
+        def move(b):
+            nc.scalar.copy(
+                out=a_grouped[b][:].bitcast(F32).rearrange("p (i u) -> p i u", u=HALVES),
+                in_=adj_turned[b][:].rearrange("p u i -> p i u"),
+            )
+
         def quantise_adj(b):
             nc.vector.quantize_mx(
                 out=a_codes[:, b, :].bitcast(FP8X4), scales=a_scales[:, b, :], in_=a_grouped[b][:]
             )
-
-        def adj_block(b):
-            return adj_rows[:, b, :]
 
         for t in range(last):
             turn_x(t, 0, PASSES)
             if t == W_SLOT:
                 group_weight()
             quantise_x(t, 0, PASSES)
-        turn_adj(0, adj_block(0))
-        square(0)
-        quantise_weight()
+            if t == W_SLOT:
+                quantise_weight()
         for g in range(PASSES):
             turn_x(last, g, g + 1)
             quantise_x(last, g, g + 1)
-        for b in range(1, last):
-            turn_adj(b, adj_block(b))
+        nc.tensor.matmul(out=bias_ps[:], lhsT=ones[:], rhs=bias_rows[:], start=True, stop=True)
+        nc.scalar.copy(out=bias_all[:], in_=bias_ps[:])
+        for b in range(PAIR):
+            turn_adj(b, adj_rows[:, b, :])
             square(b)
-        squared = keep.tile([P, NODES], BF16)
-        nc.vector.tensor_tensor(out=squared[:], in0=adj_block(last), in1=adj_block(last), op=ALU.mult)
+        squared = keep.tile([P, PAIR, NODES], BF16)
+        nc.vector.tensor_tensor(out=squared[:], in0=adj_rows[:, PAIR:, :], in1=adj_rows[:, PAIR:, :], op=ALU.mult)
         quantise_adj(0)
 
         sup_ps = sums.tile([P, TILES, OUT_F], F32)
@@ -183,12 +186,9 @@ def tile_netgraphconvolution_s_kernel(tc, x, adj, weight, bias, out):
                     start=(g == 0),
                     stop=(g == PASSES - 1),
                 )
-        nc.tensor.matmul(out=bias_ps[:], lhsT=ones[:], rhs=bias_rows[:], start=True, stop=True)
-        turn_adj(last, squared[:])
-        nc.scalar.copy(
-            out=a_grouped[last][:].bitcast(F32).rearrange("p (i u) -> p i u", u=HALVES),
-            in_=adj_turned[last][:].rearrange("p u i -> p i u"),
-        )
+        for b in range(PAIR, TILES):
+            turn_adj(b, squared[:, b - PAIR, :])
+            move(b)
         sup_grouped = keep.tile([P, OUT_F, PACK], BF16, align_bytes=64)
         nc.vector.tensor_copy(out=sup_grouped[:], in_=sup_ps[:].rearrange("p t f -> p f t"))
         quantise_adj(1)
@@ -201,7 +201,6 @@ def tile_netgraphconvolution_s_kernel(tc, x, adj, weight, bias, out):
         )
 
         quantise_adj(2)
-        nc.vector.tensor_copy(out=bias_all[:], in_=bias_ps[:])
         quantise_adj(3)
 
         out_blocks = out.rearrange("(p b) f -> p b f", b=TILES)

@@ -74,8 +74,8 @@ def tile_netgraphconvolution_s_kernel(tc, x, adj, weight, bias, out):
         )
         load_x(last)
         nc.sync.dma_start(out=bias_rows[0:1, :], in_=bias.rearrange("(o f) -> o f", o=1))
-        for h in range(TILES // PAIR):
-            load_adj(slice(PAIR * h, PAIR * h + PAIR))
+        for blocks in (slice(0, 1), slice(1, PAIR), slice(PAIR, TILES)):
+            load_adj(blocks)
 
         w_grouped = keep.tile([P, PASSES, OUT_F, PACK], BF16, align_bytes=64)
         w_codes = keep.tile([P, PASSES, OUT_F], U32, align_bytes=64)
@@ -118,8 +118,6 @@ def tile_netgraphconvolution_s_kernel(tc, x, adj, weight, bias, out):
                 in_=x_grouped[t][:, g0 * P * PACK : g1 * P * PACK],
             )
 
-        bias_ps = sums.tile([P, OUT_F], F32)
-        bias_all = keep.tile([P, OUT_F], F32)
 
         a_codes = keep.tile([P, TILES, P], U32, align_bytes=64)
         a_scales = keep.tile([P, TILES, P], U8, align_bytes=64)
@@ -165,20 +163,22 @@ def tile_netgraphconvolution_s_kernel(tc, x, adj, weight, bias, out):
         for g in range(PASSES):
             turn_x(last, g, g + 1)
             quantise_x(last, g, g + 1)
-        nc.tensor.matmul(out=bias_ps[:], lhsT=ones[:], rhs=bias_rows[:], start=True, stop=True)
-        nc.scalar.copy(out=bias_all[:], in_=bias_ps[:])
         for b in range(PAIR):
             turn_adj(b, adj_rows[:, b, :])
             square(b)
         squared = keep.tile([P, PAIR, NODES], BF16)
-        nc.vector.tensor_tensor(out=squared[:], in0=adj_rows[:, PAIR:, :], in1=adj_rows[:, PAIR:, :], op=ALU.mult)
-        quantise_adj(0)
+        for b in range(PAIR, TILES):
+            rows = adj_rows[:, b, :]
+            nc.vector.tensor_tensor(out=squared[:, b - PAIR, :], in0=rows, in1=rows, op=ALU.mult)
 
-        sup_ps = sums.tile([P, TILES, OUT_F], F32)
+        sup_ps = []
+        for h in range(TILES // PAIR):
+            sup_h = sums.tile([P, PAIR, OUT_F], F32, name="sup_ps%d" % h)
+            sup_ps.append(sup_h)
         for t in range(TILES):
             for g in range(PASSES):
                 nc.tensor.matmul_mx(
-                    out=sup_ps[:, t, :],
+                    out=sup_ps[t // PAIR][:, t % PAIR, :],
                     lhsT=x_codes[:, t, g, :].bitcast(FP8X4),
                     lhsT_scale=x_scales[:, t, g, :],
                     rhs=w_codes[:, g, :].bitcast(FP8X4),
@@ -186,12 +186,17 @@ def tile_netgraphconvolution_s_kernel(tc, x, adj, weight, bias, out):
                     start=(g == 0),
                     stop=(g == PASSES - 1),
                 )
+        sup_grouped = keep.tile([P, OUT_F, PACK], BF16, align_bytes=64)
+        nc.vector.tensor_copy(out=sup_grouped[:, :, :PAIR], in_=sup_ps[0][:].rearrange("p t f -> p f t"))
+        nc.scalar.copy(out=sup_grouped[:, :, PAIR:], in_=sup_ps[1][:].rearrange("p t f -> p f t"))
+        quantise_adj(0)
         for b in range(PAIR, TILES):
             turn_adj(b, squared[:, b - PAIR, :])
             move(b)
-        sup_grouped = keep.tile([P, OUT_F, PACK], BF16, align_bytes=64)
-        nc.vector.tensor_copy(out=sup_grouped[:], in_=sup_ps[:].rearrange("p t f -> p f t"))
-        quantise_adj(1)
+        bias_ps = turned.tile([P, OUT_F], F32, tag="turned")
+        nc.tensor.matmul(out=bias_ps[:], lhsT=ones[:], rhs=bias_rows[:], start=True, stop=True)
+        bias_all = keep.tile([P, OUT_F], F32)
+        nc.scalar.copy(out=bias_all[:], in_=bias_ps[:])
         sup_codes = keep.tile([P, OUT_F], U32, align_bytes=64)
         sup_scales = keep.tile([P, OUT_F], U8, align_bytes=64)
         nc.vector.quantize_mx(
@@ -200,8 +205,8 @@ def tile_netgraphconvolution_s_kernel(tc, x, adj, weight, bias, out):
             in_=sup_grouped[:].rearrange("p f t -> p (f t)"),
         )
 
-        quantise_adj(2)
-        quantise_adj(3)
+        for b in range(1, TILES):
+            quantise_adj(b)
 
         out_blocks = out.rearrange("(p b) f -> p b f", b=TILES)
         z = []

@@ -33,7 +33,7 @@ def tile_netgraphconvolution_s_kernel(tc, x, adj, weight, bias, out):
     with ExitStack() as ctx:
         keep = ctx.enter_context(tc.tile_pool(name="keep", bufs=1))
         turned = ctx.enter_context(tc.psum_pool(name="turned", bufs=4))
-        sums = ctx.enter_context(tc.psum_pool(name="sums", bufs=1))
+        sums = ctx.enter_context(tc.psum_pool(name="sums", bufs=4))
         ctx.enter_context(tc.manual_schedule())
 
         ident = keep.tile([P, P], F32)
@@ -173,7 +173,7 @@ def tile_netgraphconvolution_s_kernel(tc, x, adj, weight, bias, out):
 
         sup_ps = []
         for h in range(TILES // PAIR):
-            sup_h = sums.tile([P, PAIR, OUT_F], F32, name="sup_ps%d" % h)
+            sup_h = sums.tile([P, PAIR, OUT_F], F32, tag="sums", name="sup_ps%d" % h)
             sup_ps.append(sup_h)
         for t in range(TILES):
             for g in range(PASSES):
@@ -212,9 +212,15 @@ def tile_netgraphconvolution_s_kernel(tc, x, adj, weight, bias, out):
         z = []
         e = []
         for h in range(TILES // PAIR):
-            out_ps = sums.tile([P, PAIR, OUT_F], F32, name="out_ps%d" % h)
-            for s in range(PAIR):
-                b = PAIR * h + s
+            z_h = keep.tile([P, PAIR, OUT_F], F32, name="z%d" % h)
+            e_h = keep.tile([P, PAIR, OUT_F], F32, name="e%d" % h)
+            z.append(z_h)
+            e.append(e_h)
+        for b0, count in ((0, PAIR), (PAIR, 1), (last, 1)):
+            h, s0 = divmod(b0, PAIR)
+            out_ps = sums.tile([P, count, OUT_F], F32, tag="sums", name="out_ps%d" % b0)
+            for s in range(count):
+                b = b0 + s
                 nc.tensor.matmul_mx(
                     out=out_ps[:, s, :],
                     lhsT=a_codes[:, b, :].bitcast(FP8X4),
@@ -224,14 +230,14 @@ def tile_netgraphconvolution_s_kernel(tc, x, adj, weight, bias, out):
                     start=True,
                     stop=True,
                 )
-            z_h = keep.tile([P, PAIR, OUT_F], F32, name="z%d" % h)
+            part = slice(s0, s0 + count)
             nc.vector.tensor_tensor(
-                out=z_h[:], in0=out_ps[:], in1=bias_all[:].unsqueeze(1).to_broadcast([P, PAIR, OUT_F]), op=ALU.add
+                out=z[h][:, part, :],
+                in0=out_ps[:],
+                in1=bias_all[:].unsqueeze(1).to_broadcast([P, count, OUT_F]),
+                op=ALU.add,
             )
-            e_h = keep.tile([P, PAIR, OUT_F], F32, name="e%d" % h)
-            nc.scalar.activation(out=e_h[:], in_=z_h[:], func=ACT.Exp)
-            z.append(z_h)
-            e.append(e_h)
+            nc.scalar.activation(out=e[h][:, part, :], in_=z[h][:, part, :], func=ACT.Exp)
         r = []
         for h in range(TILES // PAIR):
             r_h = keep.tile([P, PAIR, OUT_F], F32, name="r%d" % h)

from contextlib import ExitStack

import concourse.mybir as mybir
from concourse.masks import make_identity

F32 = mybir.dt.float32
BF16 = mybir.dt.bfloat16
U32 = mybir.dt.uint32
U8 = mybir.dt.uint8
FP8X4 = mybir.dt.float8_e4m3fn_x4
ACT = mybir.ActivationFunctionType
ALU = mybir.AluOpType

P = 128
PACK = 4
HALVES = 2
PAIR = 2
NODES = 512
IN_F = 1024
OUT_F = 128
K_PASS = P * PACK
PASSES = IN_F // K_PASS
TILES = NODES // P

W_SLOT = 1

FLOPS = 2 * NODES * IN_F * OUT_F + 2 * NODES * NODES * OUT_F


def tile_netgraphconvolution_s_kernel(tc, x, adj, weight, bias, out):
    nc = tc.nc
    last = TILES - 1
    with ExitStack() as ctx:
        keep = ctx.enter_context(tc.tile_pool(name="keep", bufs=1))
        turned = ctx.enter_context(tc.psum_pool(name="turned", bufs=4))
        sums = ctx.enter_context(tc.psum_pool(name="sums", bufs=4))
        ctx.enter_context(tc.manual_schedule())

        ident = keep.tile([P, P], F32)
        make_identity(nc, ident[:])
        warm_in = keep.tile([P, 1], F32)
        warm_out = keep.tile([P, 1], F32)
        nc.vector.memset(warm_in[:], 0.0)
        bias_rows = keep.tile([P, OUT_F], BF16)
        nc.vector.memset(bias_rows[:], 0.0)
        ones = keep.tile([P, P], BF16)
        nc.vector.memset(ones[:], 1.0)
        nc.scalar.activation(out=warm_out[:], in_=warm_in[:], func=ACT.Exp)

        x_tiles = x.rearrange("(p t) k -> t p k", t=TILES)
        x_rows = []
        for t in range(TILES):
            x_t = keep.tile([P, IN_F], BF16, name="x_rows%d" % t)
            x_rows.append(x_t)
        w_raw = keep.tile([P, PASSES, PACK, OUT_F], BF16)
        adj_blocks = adj.rearrange("(p b) j -> p b j", b=TILES)
        adj_rows = keep.tile([P, TILES, NODES], BF16)

        def load_x(t):
            pieces = 1 if 0 < t < last else PASSES
            width = IN_F // pieces
            for c in range(pieces):
                cols = slice(c * width, (c + 1) * width)
                nc.sync.dma_start(out=x_rows[t][:, cols], in_=x_tiles[t][:, cols])

        def load_adj(blocks):
            nc.sync.dma_start(out=adj_rows[:, blocks, :], in_=adj_blocks[:, blocks, :])

        for t in range(last):
            load_x(t)
        nc.sync.dma_start(
            out=w_raw[:].rearrange("p g t c -> p g (t c)"),
            in_=weight.rearrange("(g p t) c -> p g (t c)", g=PASSES, p=P),
        )
        load_x(last)
        nc.sync.dma_start(out=bias_rows[0:1, :], in_=bias.rearrange("(o f) -> o f", o=1))
        for blocks in (slice(0, 1), slice(1, PAIR), slice(PAIR, TILES)):
            load_adj(blocks)

        w_grouped = keep.tile([P, PASSES, OUT_F, PACK], BF16, align_bytes=64)
        w_codes = keep.tile([P, PASSES, OUT_F], U32, align_bytes=64)
        w_scales = keep.tile([P, PASSES, OUT_F], U8, align_bytes=64)

        def group_weight():
            nc.vector.tensor_copy(out=w_grouped[:], in_=w_raw[:].rearrange("p g t c -> p g c t"))

        def quantise_weight():
            nc.vector.quantize_mx(
                out=w_codes[:].rearrange("p g c -> p (g c)").bitcast(FP8X4),
                scales=w_scales[:].rearrange("p g c -> p (g c)"),
                in_=w_grouped[:].rearrange("p g c t -> p (g c t)"),
            )

        x_codes = keep.tile([P, TILES, PASSES, P], U32, align_bytes=64)
        x_scales = keep.tile([P, TILES, PASSES, P], U8, align_bytes=64)
        x_grouped = []
        for t in range(TILES):
            x_g = keep.tile([P, PASSES * P * PACK], BF16, name="x_grouped%d" % t, align_bytes=64)
            x_grouped.append(x_g)

        def turn_x(t, g0, g1):
            x_words = x_rows[t][:].bitcast(F32)
            xT = turned.tile([P, (g1 - g0) * HALVES, P], F32, tag="turned")
            for g in range(g0, g1):
                for u in range(HALVES):
                    first = HALVES * P * g + u
                    nc.tensor.transpose(
                        xT[:, HALVES * (g - g0) + u, :], x_words[:, first : HALVES * P * (g + 1) : HALVES], ident[:]
                    )
            grouped_words = x_grouped[t][:].bitcast(F32).rearrange("p (g n u) -> p g n u", g=PASSES, u=HALVES)
            turned_words = xT[:].rearrange("p (g u) n -> p g n u", u=HALVES)
            nc.scalar.copy(out=grouped_words[:, g0:g1], in_=turned_words)

        def quantise_x(t, g0, g1):
            nc.vector.quantize_mx(
                out=x_codes[:, t, g0:g1].rearrange("p g n -> p (g n)").bitcast(FP8X4),
                scales=x_scales[:, t, g0:g1].rearrange("p g n -> p (g n)"),
                in_=x_grouped[t][:, g0 * P * PACK : g1 * P * PACK],
            )


        a_codes = keep.tile([P, TILES, P], U32, align_bytes=64)
        a_scales = keep.tile([P, TILES, P], U8, align_bytes=64)
        adj_turned = {}

        def turn_adj(b, rows):
            aT = turned.tile([P, HALVES, P], F32, tag="turned")
            adj_words = rows.bitcast(F32)
            for u in range(HALVES):
                nc.tensor.transpose(aT[:, u, :], adj_words[:, u : HALVES * P : HALVES], ident[:])
            adj_turned[b] = aT

        a_grouped = []
        for b in range(TILES):
            a_g = keep.tile([P, P * PACK], BF16, name="a_grouped%d" % b, align_bytes=64)
            a_grouped.append(a_g)

        def square(b):
            nc.scalar.activation(
                out=a_grouped[b][:].rearrange("p (i u e) -> p i u e", u=HALVES, e=PAIR),
                in_=adj_turned[b][:].bitcast(BF16).rearrange("p u (i e) -> p i u e", e=PAIR),
                func=ACT.Square,
            )

        def move(b):
            nc.scalar.copy(
                out=a_grouped[b][:].bitcast(F32).rearrange("p (i u) -> p i u", u=HALVES),
                in_=adj_turned[b][:].rearrange("p u i -> p i u"),
            )

        def quantise_adj(b):
            nc.vector.quantize_mx(
                out=a_codes[:, b, :].bitcast(FP8X4), scales=a_scales[:, b, :], in_=a_grouped[b][:]
            )

        for t in range(last):
            turn_x(t, 0, PASSES)
            if t == W_SLOT:
                group_weight()
            quantise_x(t, 0, PASSES)
            if t == W_SLOT:
                quantise_weight()
        for g in range(PASSES):
            turn_x(last, g, g + 1)
            quantise_x(last, g, g + 1)
        for b in range(PAIR):
            turn_adj(b, adj_rows[:, b, :])
            square(b)
        squared = keep.tile([P, PAIR, NODES], BF16)
        for b in range(PAIR, TILES):
            rows = adj_rows[:, b, :]
            nc.vector.tensor_tensor(out=squared[:, b - PAIR, :], in0=rows, in1=rows, op=ALU.mult)

        sup_ps = []
        for h in range(TILES // PAIR):
            sup_h = sums.tile([P, PAIR, OUT_F], F32, tag="sums", name="sup_ps%d" % h)
            sup_ps.append(sup_h)
        for t in range(TILES):
            for g in range(PASSES):
                nc.tensor.matmul_mx(
                    out=sup_ps[t // PAIR][:, t % PAIR, :],
                    lhsT=x_codes[:, t, g, :].bitcast(FP8X4),
                    lhsT_scale=x_scales[:, t, g, :],
                    rhs=w_codes[:, g, :].bitcast(FP8X4),
                    rhs_scale=w_scales[:, g, :],
                    start=(g == 0),
                    stop=(g == PASSES - 1),
                )
        sup_grouped = keep.tile([P, OUT_F, PACK], BF16, align_bytes=64)
        nc.vector.tensor_copy(out=sup_grouped[:, :, :PAIR], in_=sup_ps[0][:].rearrange("p t f -> p f t"))
        nc.scalar.copy(out=sup_grouped[:, :, PAIR:], in_=sup_ps[1][:].rearrange("p t f -> p f t"))
        quantise_adj(0)
        for b in range(PAIR, TILES):
            turn_adj(b, squared[:, b - PAIR, :])
            move(b)
        bias_ps = turned.tile([P, OUT_F], F32, tag="turned")
        nc.tensor.matmul(out=bias_ps[:], lhsT=ones[:], rhs=bias_rows[:], start=True, stop=True)
        bias_all = keep.tile([P, OUT_F], F32)
        nc.scalar.copy(out=bias_all[:], in_=bias_ps[:])
        sup_codes = keep.tile([P, OUT_F], U32, align_bytes=64)
        sup_scales = keep.tile([P, OUT_F], U8, align_bytes=64)
        nc.vector.quantize_mx(
            out=sup_codes[:].bitcast(FP8X4),
            scales=sup_scales[:],
            in_=sup_grouped[:].rearrange("p f t -> p (f t)"),
        )

        for b in range(1, TILES):
            quantise_adj(b)

        out_blocks = out.rearrange("(p b) f -> p b f", b=TILES)
        z = []
        e = []
        for h in range(TILES // PAIR):
            z_h = keep.tile([P, PAIR, OUT_F], F32, name="z%d" % h)
            e_h = keep.tile([P, PAIR, OUT_F], F32, name="e%d" % h)
            z.append(z_h)
            e.append(e_h)
        for b0, count in ((0, PAIR), (PAIR, 1), (last, 1)):
            h, s0 = divmod(b0, PAIR)
            out_ps = sums.tile([P, count, OUT_F], F32, tag="sums", name="out_ps%d" % b0)
            for s in range(count):
                b = b0 + s
                nc.tensor.matmul_mx(
                    out=out_ps[:, s, :],
                    lhsT=a_codes[:, b, :].bitcast(FP8X4),
                    lhsT_scale=a_scales[:, b, :],
                    rhs=sup_codes[:].bitcast(FP8X4),
                    rhs_scale=sup_scales[:],
                    start=True,
                    stop=True,
                )
            part = slice(s0, s0 + count)
            nc.vector.tensor_tensor(
                out=z[h][:, part, :],
                in0=out_ps[:],
                in1=bias_all[:].unsqueeze(1).to_broadcast([P, count, OUT_F]),
                op=ALU.add,
            )
            nc.scalar.activation(out=e[h][:, part, :], in_=z[h][:, part, :], func=ACT.Exp)
        r = []
        for h in range(TILES // PAIR):
            r_h = keep.tile([P, PAIR, OUT_F], F32, name="r%d" % h)
            nc.vector.tensor_scalar(out=r_h[:], in0=z[h][:], scalar1=0.0, scalar2=-1.0, op0=ALU.max, op1=ALU.add)
            r.append(r_h)
        for h in range(TILES // PAIR):
            res = keep.tile([P, PAIR, OUT_F], F32, name="res%d" % h)
            nc.vector.scalar_tensor_tensor(
                out=res[:].rearrange("p b f -> p (b f)"),
                in0=e[h][:].rearrange("p b f -> p (b f)"),
                scalar=1.0,
                in1=r[h][:].rearrange("p b f -> p (b f)"),
                op0=ALU.min,
                op1=ALU.add,
            )
            nc.sync.dma_start(out=out_blocks[:, PAIR * h : PAIR * h + PAIR, :], in_=res[:])
